import numpy as np
import ml_dtypes


def mxq(x, axis, fmt="e4m3"):
    dtype, down = {"e4m3": (ml_dtypes.float8_e4m3fn, 7), "e5m2": (ml_dtypes.float8_e5m2, 14)}[fmt]
    v = np.moveaxis(np.asarray(x, np.float32).astype(ml_dtypes.bfloat16).astype(np.float64), axis, -1)
    blocks = v.reshape(v.shape[:-1] + (-1, 32))
    amax = np.abs(blocks).max(-1, keepdims=True)
    byte = np.maximum(np.where(amax > 0, np.frexp(amax)[1] - 1 + 127, 0) - down, 1)
    scale = np.exp2(byte - 127.0)
    codes = (blocks / scale).astype(np.float32).astype(dtype).astype(np.float64)
    return np.moveaxis((codes * scale).reshape(v.shape), -1, axis)


WIDE = False


def mx_kscale(k):
    if not WIDE:
        return np.ones(k)
    levels = np.array([10, -10, 5, -5, 0])
    if k % 512:
        return np.exp2(np.random.permutation(np.resize(levels, k // 32))).repeat(32)
    a = np.empty((k // 512, 16))
    for p in range(k // 512):
        a[p, :8] = np.random.permutation(np.resize(levels, 8))
        for g in range(8):
            far = levels[np.abs(levels - a[p, g]) >= 10]
            a[p, g + 8] = far[np.random.randint(len(far))]
    return np.exp2(a.ravel()).repeat(32)


BF16 = ml_dtypes.bfloat16


def bf(x):
    return np.asarray(x, np.float32).astype(BF16)


def f64(x):
    return np.asarray(x).astype(np.float64)


B, S, HID, H, G, D, QB = 4, 2048, 1024, 2, 1, 128, 512
ROPE_THETA = 1.0e6


def rotate_half(t):
    t1 = t[..., t.shape[-1] // 2:]
    t2 = t[..., : t.shape[-1] // 2]
    return np.concatenate((-t1, t2), axis=-1)


def rope_tables():
    inv_freq = 1.0 / (ROPE_THETA ** (np.arange(0, D, 2) / D))
    freqs = np.arange(S)[:, None] * inv_freq[None, :]
    emb = np.concatenate((freqs, freqs), axis=-1)
    return np.cos(emb), np.sin(emb)


def setup_inputs():
    s = mx_kscale(HID)
    cos, sin = rope_tables()
    return {"x": bf(np.random.standard_normal((B, S, HID)) * s),
            "cos": bf(cos),
            "sin": bf(sin),
            "Wq": bf(np.random.standard_normal((HID, H * D)) * 1.5 / np.sqrt(HID) / s[:, None]),
            "Wk": bf(np.random.standard_normal((HID, G * D)) * 1.5 / np.sqrt(HID) / s[:, None]),
            "Wv": bf(np.random.standard_normal((HID, G * D)) * 1.0 / np.sqrt(HID) / s[:, None])}


def reference(x, cos, sin, Wq, Wk, Wv):
    xq = mxq(f64(x), 2, "e4m3")
    q = (xq @ mxq(f64(Wq), 0, "e4m3")).reshape(B, S, H, D)
    k = (xq @ mxq(f64(Wk), 0, "e4m3")).reshape(B, S, G, D)
    v = (xq @ mxq(f64(Wv), 0, "e4m3")).reshape(B, S, G, D)
    c = f64(cos)[None, :, None, :]
    sn = f64(sin)[None, :, None, :]
    q = q * c + rotate_half(q) * sn
    k = k * c + rotate_half(k) * sn
    return q, k, v

@@ -1,0 +1,203 @@
+from contextlib import ExitStack
+
+import concourse.mybir as mybir
+from concourse.masks import make_identity
+
+F32 = mybir.dt.float32
+BF16 = mybir.dt.bfloat16
+U32 = mybir.dt.uint32
+U8 = mybir.dt.uint8
+FP8X4 = mybir.dt.float8_e4m3fn_x4
+ALU = mybir.AluOpType
+
+P = 128
+BATCH, SEQ, HID = 4, 2048, 1024
+HEAD = 128
+HALF = HEAD // 2
+Q_HEADS = 2
+ROT_HEADS = Q_HEADS + 1
+HEADS = ROT_HEADS + 1
+OUT_COLS = HEADS * HEAD
+
+PACK = 4
+PASSES = HID // (P * PACK)
+PAIR = 2
+
+TILES = 4
+CHUNKS = BATCH * SEQ // (TILES * P)
+SEQ_CHUNKS = SEQ // (TILES * P)
+Q_VECTORS = TILES * Q_HEADS
+ROT_VECTORS = TILES * ROT_HEADS
+
+LOAD_AHEAD = 4
+X_BUFS = LOAD_AHEAD + 2
+
+FLOPS = 2 * BATCH * SEQ * HID * OUT_COLS
+
+
+def tile_attention_pa_t_kernel(tc, x, cos, sin, Wq, Wk, Wv, out_0, out_1, out_2):
+    nc = tc.nc
+
+    by_chunk = "(c p j) n -> c p (j n)"
+    x_chunks = x.flatten_outer_dims().rearrange(by_chunk, p=P, j=TILES)
+    q_chunks = out_0.rearrange("b s h d -> (b s) (h d)").rearrange(by_chunk, p=P, j=TILES)
+    k_chunks = out_1.rearrange("b s h d -> (b s) (h d)").rearrange(by_chunk, p=P, j=TILES)
+    v_chunks = out_2.rearrange("b s h d -> (b s) (h d)").rearrange(by_chunk, p=P, j=TILES)
+
+    with ExitStack() as stack:
+        stack.enter_context(tc.manual_schedule())
+        const = stack.enter_context(tc.tile_pool(name="const", bufs=1))
+        x_pool = stack.enter_context(tc.tile_pool(name="x", bufs=X_BUFS))
+        mx_pool = stack.enter_context(tc.tile_pool(name="mx", bufs=2))
+        out_pool = stack.enter_context(tc.tile_pool(name="out", bufs=3))
+        xt_psum = stack.enter_context(tc.psum_pool(name="xt_psum", bufs=TILES))
+        head_psum = stack.enter_context(tc.psum_pool(name="head_psum", bufs=1))
+
+        x_tiles, grouped_tiles, code_tiles, scale_tiles, head_tiles = {}, {}, {}, {}, {}
+
+        def load(c, pieces=1):
+            x_sb = x_pool.tile([P, TILES * HID], BF16, name="x_sb")
+            width = TILES * HID // pieces
+            for i in range(pieces):
+                columns = slice(i * width, (i + 1) * width)
+                nc.sync.dma_start(out=x_sb[:, columns], in_=x_chunks[c][:, columns])
+            x_tiles[c] = x_sb
+
+        def transpose(c):
+            x_words = x_tiles[c][:].bitcast(F32)
+            grouped = mx_pool.tile([P, TILES * HID], BF16, name="grouped", align_bytes=64)
+            grouped_words = grouped[:].bitcast(F32).rearrange(
+                "p (j g r u) -> p j g r u", j=TILES, g=PASSES, u=PAIR
+            )
+            for j in range(TILES):
+                xt = xt_psum.tile([P, PASSES, PAIR, P], F32, name="xt")
+                for g in range(PASSES):
+                    for u in range(PAIR):
+                        first = (j * PASSES + g) * PAIR * P
+                        nc.tensor.transpose(
+                            out=xt[:, g, u, :],
+                            in_=x_words[:, first + u : first + PAIR * P : PAIR],
+                            identity=ident[:],
+                        )
+                nc.scalar.copy(out=grouped_words[:, j], in_=xt[:].rearrange("p g u r -> p g r u"))
+            grouped_tiles[c] = grouped
+
+        def quantise(c):
+            x_codes = mx_pool.tile([P, TILES * PASSES * P], U32, name="x_codes", align_bytes=64)
+            x_scales = mx_pool.tile([P, TILES * PASSES * P], U8, name="x_scales", align_bytes=64)
+            nc.vector.quantize_mx(
+                out=x_codes[:].bitcast(FP8X4), scales=x_scales[:], in_=grouped_tiles[c][:]
+            )
+            code_tiles[c], scale_tiles[c] = x_codes, x_scales
+
+        def project(c, h):
+            acc = head_psum.tile([P, TILES, HEAD], F32, name="head%d" % h)
+            for j in range(TILES):
+                for g in range(PASSES):
+                    tokens = slice((j * PASSES + g) * P, (j * PASSES + g + 1) * P)
+                    columns = slice(g * OUT_COLS + h * HEAD, g * OUT_COLS + (h + 1) * HEAD)
+                    nc.tensor.matmul_mx(
+                        out=acc[:, j, :],
+                        lhsT=code_tiles[c][:, tokens].bitcast(FP8X4),
+                        lhsT_scale=scale_tiles[c][:, tokens],
+                        rhs=w_codes[:, columns].bitcast(FP8X4),
+                        rhs_scale=w_scales[:, columns],
+                        start=(g == 0),
+                        stop=(g == PASSES - 1),
+                    )
+            head_tiles[c, h] = acc
+
+        def rotate_and_store(c):
+            v_out = out_pool.tile([P, TILES, HEAD], F32, name="v_out")
+            nc.scalar.copy(out=v_out[:], in_=head_tiles[c, ROT_HEADS][:])
+            nc.sync.dma_start(out=v_chunks[c], in_=v_out[:].rearrange("p j d -> p (j d)"))
+
+            products = out_pool.tile([P, 2, ROT_VECTORS, HEAD], F32, name="products")
+            q_products = products[:, :, 0:Q_VECTORS, :].rearrange("p w (j h) d -> p w j h d", h=Q_HEADS)
+            first = (c % SEQ_CHUNKS) * TILES
+            for h in range(ROT_HEADS):
+                nc.vector.tensor_tensor(
+                    out=(
+                        q_products[:, :, :, h, :]
+                        if h < Q_HEADS
+                        else products[:, :, Q_VECTORS:ROT_VECTORS, :]
+                    ),
+                    in0=head_tiles[c, h][:].unsqueeze(1).to_broadcast([P, 2, TILES, HEAD]),
+                    in1=tables[:, :, first : first + TILES, :],
+                    op=ALU.mult,
+                )
+
+            adder = nc.gpsimd if c < CHUNKS - 1 else nc.vector
+            rot, cross = products[:, 0], products[:, 1]
+            adder.tensor_tensor(
+                out=rot[:, :, 0:HALF], in0=rot[:, :, 0:HALF], in1=cross[:, :, HALF:HEAD], op=ALU.subtract
+            )
+            adder.tensor_tensor(
+                out=rot[:, :, HALF:HEAD], in0=rot[:, :, HALF:HEAD], in1=cross[:, :, 0:HALF], op=ALU.add
+            )
+            nc.sync.dma_start(out=q_chunks[c], in_=rot[:, 0:Q_VECTORS, :].rearrange("p n d -> p (n d)"))
+            nc.sync.dma_start(
+                out=k_chunks[c], in_=rot[:, Q_VECTORS:ROT_VECTORS, :].rearrange("p n d -> p (n d)")
+            )
+
+        ident = const.tile([P, P], F32)
+        make_identity(nc, ident[:])
+
+        w_raws = []
+        for name, w in (("wq_raw", Wq), ("wk_raw", Wk), ("wv_raw", Wv)):
+            w_raw = const.tile([P, PASSES, PACK, w.shape[1]], BF16, name=name)
+            nc.sync.dma_start(
+                out=w_raw[:].rearrange("p g t n -> p g (t n)"),
+                in_=w.rearrange("(g q t) n -> q g (t n)", q=P, t=PACK),
+            )
+            w_raws.append((w_raw, w.shape[1]))
+
+        load(0, pieces=TILES)
+
+        tables = const.tile([P, 2, SEQ_CHUNKS * TILES, HEAD], BF16)
+        sin_sb = const.tile([P, SEQ_CHUNKS * TILES, HEAD], BF16)
+        for table_sb, table in ((sin_sb[:], sin), (tables[:, 0], cos)):
+            nc.sync.dma_start(
+                out=table_sb.rearrange("p (c j) d -> p c (j d)", j=TILES),
+                in_=table.rearrange("(c p j) d -> p c (j d)", p=P, j=TILES),
+            )
+
+        for c in range(1, LOAD_AHEAD):
+            load(c)
+
+        w_grouped = const.tile([P, PASSES, OUT_COLS, PACK], BF16, align_bytes=64)
+        w_first = 0
+        for w_raw, w_cols in w_raws:
+            for g in range(PASSES):
+                nc.vector.tensor_copy(
+                    out=w_grouped[:, g, w_first : w_first + w_cols, :],
+                    in_=w_raw[:, g].rearrange("p t n -> p n t"),
+                )
+            w_first += w_cols
+        w_codes = const.tile([P, PASSES * OUT_COLS], U32, align_bytes=64)
+        w_scales = const.tile([P, PASSES * OUT_COLS], U8, align_bytes=64)
+        nc.vector.quantize_mx(
+            out=w_codes[:].bitcast(FP8X4),
+            scales=w_scales[:],
+            in_=w_grouped[:].rearrange("p g n t -> p (g n t)"),
+        )
+
+        transpose(0)
+        transpose(1)
+
+        nc.scalar.copy(out=tables[:, 1, :, 0:HALF], in_=sin_sb[:, :, HALF:HEAD])
+        nc.scalar.copy(out=tables[:, 1, :, HALF:HEAD], in_=sin_sb[:, :, 0:HALF])
+
+        quantise(0)
+        for c in range(CHUNKS):
+            if c + LOAD_AHEAD < CHUNKS:
+                load(c + LOAD_AHEAD)
+            if c + 1 < CHUNKS:
+                quantise(c + 1)
+            for h in range(Q_HEADS):
+                project(c, h)
+            if c + 2 < CHUNKS:
+                transpose(c + 2)
+            for h in range(Q_HEADS, HEADS):
+                project(c, h)
+            rotate_and_store(c)

@@ -128,12 +128,11 @@ def tile_attention_pa_t_kernel(tc, x, cos, sin, Wq, Wk, Wv, out_0, out_1, out_2)
                 )
 
             adder = nc.gpsimd if c < CHUNKS - 1 else nc.vector
-            rot, cross = products[:, 0], products[:, 1]
+            rot = products[:, 0]
+            rot_halves = rot.rearrange("p n (f d) -> p n f d", f=2)
+            cross_halves = products[:, 1].rearrange("p n (f d) -> p n f d", f=2)
             adder.tensor_tensor(
-                out=rot[:, :, 0:HALF], in0=rot[:, :, 0:HALF], in1=cross[:, :, HALF:HEAD], op=ALU.subtract
-            )
-            adder.tensor_tensor(
-                out=rot[:, :, HALF:HEAD], in0=rot[:, :, HALF:HEAD], in1=cross[:, :, 0:HALF], op=ALU.add
+                out=rot_halves, in0=rot_halves, in1=cross_halves[:, :, ::-1, :], op=ALU.add
             )
             nc.sync.dma_start(out=q_chunks[c], in_=rot[:, 0:Q_VECTORS, :].rearrange("p n d -> p (n d)"))
             nc.sync.dma_start(
@@ -186,7 +185,7 @@ def tile_attention_pa_t_kernel(tc, x, cos, sin, Wq, Wk, Wv, out_0, out_1, out_2)
         transpose(1)
 
         nc.scalar.copy(out=tables[:, 1, :, 0:HALF], in_=sin_sb[:, :, HALF:HEAD])
-        nc.scalar.copy(out=tables[:, 1, :, HALF:HEAD], in_=sin_sb[:, :, 0:HALF])
+        nc.scalar.mul(tables[:, 1, :, HALF:HEAD], sin_sb[:, :, 0:HALF], -1.0)
 
         quantise(0)
         for c in range(CHUNKS):

@@ -24,6 +24,8 @@ PASSES = HID // (P * PACK)
 PAIR = 2
 
 TILES = 4
+Q_BANK_TILES = 2
+Q_BANKS = TILES // Q_BANK_TILES
 CHUNKS = BATCH * SEQ // (TILES * P)
 SEQ_CHUNKS = SEQ // (TILES * P)
 Q_VECTORS = TILES * Q_HEADS
@@ -53,7 +55,7 @@ def tile_attention_pa_t_kernel(tc, x, cos, sin, Wq, Wk, Wv, out_0, out_1, out_2)
         xt_psum = stack.enter_context(tc.psum_pool(name="xt_psum", bufs=TILES))
         head_psum = stack.enter_context(tc.psum_pool(name="head_psum", bufs=1))
 
-        x_tiles, grouped_tiles, code_tiles, scale_tiles, head_tiles = {}, {}, {}, {}, {}
+        x_tiles, grouped_tiles, code_tiles, scale_tiles, head_tiles, product_tiles = {}, {}, {}, {}, {}, {}
 
         def load(c, pieces=1):
             x_sb = x_pool.tile([P, TILES * HID], BF16, name="x_sb")
@@ -90,14 +92,14 @@ def tile_attention_pa_t_kernel(tc, x, cos, sin, Wq, Wk, Wv, out_0, out_1, out_2)
             )
             code_tiles[c], scale_tiles[c] = x_codes, x_scales
 
-        def project(c, h):
-            acc = head_psum.tile([P, TILES, HEAD], F32, name="head%d" % h)
-            for j in range(TILES):
+        def project(c, name, tiles, first_col, cols):
+            acc = head_psum.tile([P, len(tiles) * cols], F32, name=name)
+            for i, j in enumerate(tiles):
                 for g in range(PASSES):
                     tokens = slice((j * PASSES + g) * P, (j * PASSES + g + 1) * P)
-                    columns = slice(g * OUT_COLS + h * HEAD, g * OUT_COLS + (h + 1) * HEAD)
+                    columns = slice(g * OUT_COLS + first_col, g * OUT_COLS + first_col + cols)
                     nc.tensor.matmul_mx(
-                        out=acc[:, j, :],
+                        out=acc[:, i * cols : (i + 1) * cols],
                         lhsT=code_tiles[c][:, tokens].bitcast(FP8X4),
                         lhsT_scale=scale_tiles[c][:, tokens],
                         rhs=w_codes[:, columns].bitcast(FP8X4),
@@ -105,35 +107,56 @@ def tile_attention_pa_t_kernel(tc, x, cos, sin, Wq, Wk, Wv, out_0, out_1, out_2)
                         start=(g == 0),
                         stop=(g == PASSES - 1),
                     )
-            head_tiles[c, h] = acc
+            head_tiles[c, name] = acc
 
-        def rotate_and_store(c):
-            v_out = out_pool.tile([P, TILES, HEAD], F32, name="v_out")
-            nc.scalar.copy(out=v_out[:], in_=head_tiles[c, ROT_HEADS][:])
-            nc.sync.dma_start(out=v_chunks[c], in_=v_out[:].rearrange("p j d -> p (j d)"))
+        def project_q(c):
+            for b in range(Q_BANKS):
+                tiles = range(b * Q_BANK_TILES, (b + 1) * Q_BANK_TILES)
+                project(c, "q%d" % b, tiles, 0, Q_HEADS * HEAD)
 
+        def project_kv(c):
+            for name, first_head in (("k", Q_HEADS), ("v", ROT_HEADS)):
+                project(c, name, range(TILES), first_head * HEAD, HEAD)
+
+        def store_v(c):
+            v_out = out_pool.tile([P, TILES * HEAD], F32, name="v_out")
+            nc.scalar.copy(out=v_out[:], in_=head_tiles[c, "v"][:])
+            nc.sync.dma_start(out=v_chunks[c], in_=v_out[:])
+
+        def multiply(c):
             products = out_pool.tile([P, 2, ROT_VECTORS, HEAD], F32, name="products")
-            q_products = products[:, :, 0:Q_VECTORS, :].rearrange("p w (j h) d -> p w j h d", h=Q_HEADS)
             first = (c % SEQ_CHUNKS) * TILES
-            for h in range(ROT_HEADS):
+            vectors = Q_BANK_TILES * Q_HEADS
+            for b in range(Q_BANKS):
+                tile0 = first + b * Q_BANK_TILES
                 nc.vector.tensor_tensor(
-                    out=(
-                        q_products[:, :, :, h, :]
-                        if h < Q_HEADS
-                        else products[:, :, Q_VECTORS:ROT_VECTORS, :]
-                    ),
-                    in0=head_tiles[c, h][:].unsqueeze(1).to_broadcast([P, 2, TILES, HEAD]),
-                    in1=tables[:, :, first : first + TILES, :],
+                    out=products[:, :, b * vectors : (b + 1) * vectors, :].rearrange("p w n d -> p w (n d)"),
+                    in0=head_tiles[c, "q%d" % b][:].unsqueeze(1).to_broadcast([P, 2, vectors * HEAD]),
+                    in1=tables[:, :, tile0 : tile0 + Q_BANK_TILES, :, :].rearrange("p w j h d -> p w (j h d)"),
                     op=ALU.mult,
                 )
+            nc.vector.tensor_tensor(
+                out=products[:, :, Q_VECTORS:ROT_VECTORS, :],
+                in0=head_tiles[c, "k"][:]
+                .rearrange("p (j d) -> p j d", d=HEAD)
+                .unsqueeze(1)
+                .to_broadcast([P, 2, TILES, HEAD]),
+                in1=tables[:, :, first : first + TILES, 0, :],
+                op=ALU.mult,
+            )
+            product_tiles[c] = products
 
+        def add(c):
             adder = nc.gpsimd if c < CHUNKS - 1 else nc.vector
-            rot = products[:, 0]
+            rot = product_tiles[c][:, 0]
             rot_halves = rot.rearrange("p n (f d) -> p n f d", f=2)
-            cross_halves = products[:, 1].rearrange("p n (f d) -> p n f d", f=2)
+            cross_halves = product_tiles[c][:, 1].rearrange("p n (f d) -> p n f d", f=2)
             adder.tensor_tensor(
                 out=rot_halves, in0=rot_halves, in1=cross_halves[:, :, ::-1, :], op=ALU.add
             )
+
+        def store_qk(c):
+            rot = product_tiles[c][:, 0]
             nc.sync.dma_start(out=q_chunks[c], in_=rot[:, 0:Q_VECTORS, :].rearrange("p n d -> p (n d)"))
             nc.sync.dma_start(
                 out=k_chunks[c], in_=rot[:, Q_VECTORS:ROT_VECTORS, :].rearrange("p n d -> p (n d)")
@@ -153,11 +176,11 @@ def tile_attention_pa_t_kernel(tc, x, cos, sin, Wq, Wk, Wv, out_0, out_1, out_2)
 
         load(0, pieces=TILES)
 
-        tables = const.tile([P, 2, SEQ_CHUNKS * TILES, HEAD], BF16)
         sin_sb = const.tile([P, SEQ_CHUNKS * TILES, HEAD], BF16)
-        for table_sb, table in ((sin_sb[:], sin), (tables[:, 0], cos)):
+        cos_sb = const.tile([P, SEQ_CHUNKS * TILES, HEAD], BF16)
+        for table_sb, table in ((sin_sb, sin), (cos_sb, cos)):
             nc.sync.dma_start(
-                out=table_sb.rearrange("p (c j) d -> p c (j d)", j=TILES),
+                out=table_sb[:].rearrange("p (c j) d -> p c (j d)", j=TILES),
                 in_=table.rearrange("(c p j) d -> p c (j d)", p=P, j=TILES),
             )
 
@@ -184,8 +207,14 @@ def tile_attention_pa_t_kernel(tc, x, cos, sin, Wq, Wk, Wv, out_0, out_1, out_2)
         transpose(0)
         transpose(1)
 
-        nc.scalar.copy(out=tables[:, 1, :, 0:HALF], in_=sin_sb[:, :, HALF:HEAD])
-        nc.scalar.mul(tables[:, 1, :, HALF:HEAD], sin_sb[:, :, 0:HALF], -1.0)
+        tables = const.tile([P, 2, SEQ_CHUNKS * TILES, Q_HEADS, HEAD], BF16)
+        for c in range(SEQ_CHUNKS):
+            rows = slice(c * TILES, (c + 1) * TILES)
+            cos_rows = cos_sb[:, rows, :].unsqueeze(2).to_broadcast([P, TILES, Q_HEADS, HEAD])
+            sin_rows = sin_sb[:, rows, :].unsqueeze(2).to_broadcast([P, TILES, Q_HEADS, HEAD])
+            nc.scalar.copy(out=tables[:, 0, rows, :, :], in_=cos_rows)
+            nc.scalar.copy(out=tables[:, 1, rows, :, 0:HALF], in_=sin_rows[:, :, :, HALF:HEAD])
+            nc.scalar.mul(tables[:, 1, rows, :, HALF:HEAD], sin_rows[:, :, :, 0:HALF], -1.0)
 
         quantise(0)
         for c in range(CHUNKS):
@@ -193,10 +222,13 @@ def tile_attention_pa_t_kernel(tc, x, cos, sin, Wq, Wk, Wv, out_0, out_1, out_2)
                 load(c + LOAD_AHEAD)
             if c + 1 < CHUNKS:
                 quantise(c + 1)
-            for h in range(Q_HEADS):
-                project(c, h)
+            project_q(c)
+            project_kv(c)
+            store_v(c)
             if c + 2 < CHUNKS:
                 transpose(c + 2)
-            for h in range(Q_HEADS, HEADS):
-                project(c, h)
-            rotate_and_store(c)
+            multiply(c)
+            add(c)
+            if c > 0:
+                store_qk(c - 1)
+        store_qk(CHUNKS - 1)

@@ -56,6 +56,7 @@ def tile_attention_pa_t_kernel(tc, x, cos, sin, Wq, Wk, Wv, out_0, out_1, out_2)
         head_psum = stack.enter_context(tc.psum_pool(name="head_psum", bufs=1))
 
         x_tiles, grouped_tiles, code_tiles, scale_tiles, head_tiles, product_tiles = {}, {}, {}, {}, {}, {}
+        w_operands = {}
 
         def load(c, pieces=1):
             x_sb = x_pool.tile([P, TILES * HID], BF16, name="x_sb")
@@ -84,20 +85,26 @@ def tile_attention_pa_t_kernel(tc, x, cos, sin, Wq, Wk, Wv, out_0, out_1, out_2)
                 nc.scalar.copy(out=grouped_words[:, j], in_=xt[:].rearrange("p g u r -> p g r u"))
             grouped_tiles[c] = grouped
 
-        def quantise(c):
+        def quantise(c, pieces=1):
             x_codes = mx_pool.tile([P, TILES * PASSES * P], U32, name="x_codes", align_bytes=64)
             x_scales = mx_pool.tile([P, TILES * PASSES * P], U8, name="x_scales", align_bytes=64)
-            nc.vector.quantize_mx(
-                out=x_codes[:].bitcast(FP8X4), scales=x_scales[:], in_=grouped_tiles[c][:]
-            )
+            words = TILES * PASSES * P // pieces
+            for i in range(pieces):
+                columns = slice(i * words, (i + 1) * words)
+                nc.vector.quantize_mx(
+                    out=x_codes[:, columns].bitcast(FP8X4),
+                    scales=x_scales[:, columns],
+                    in_=grouped_tiles[c][:, i * words * PACK : (i + 1) * words * PACK],
+                )
             code_tiles[c], scale_tiles[c] = x_codes, x_scales
 
-        def project(c, name, tiles, first_col, cols):
+        def project(c, name, tiles, weight):
+            w_codes, w_scales, cols = w_operands[weight]
             acc = head_psum.tile([P, len(tiles) * cols], F32, name=name)
             for i, j in enumerate(tiles):
                 for g in range(PASSES):
                     tokens = slice((j * PASSES + g) * P, (j * PASSES + g + 1) * P)
-                    columns = slice(g * OUT_COLS + first_col, g * OUT_COLS + first_col + cols)
+                    columns = slice(g * cols, (g + 1) * cols)
                     nc.tensor.matmul_mx(
                         out=acc[:, i * cols : (i + 1) * cols],
                         lhsT=code_tiles[c][:, tokens].bitcast(FP8X4),
@@ -112,18 +119,18 @@ def tile_attention_pa_t_kernel(tc, x, cos, sin, Wq, Wk, Wv, out_0, out_1, out_2)
         def project_q(c):
             for b in range(Q_BANKS):
                 tiles = range(b * Q_BANK_TILES, (b + 1) * Q_BANK_TILES)
-                project(c, "q%d" % b, tiles, 0, Q_HEADS * HEAD)
+                project(c, "q%d" % b, tiles, "q")
 
         def project_kv(c):
-            for name, first_head in (("k", Q_HEADS), ("v", ROT_HEADS)):
-                project(c, name, range(TILES), first_head * HEAD, HEAD)
+            for name in ("k", "v"):
+                project(c, name, range(TILES), name)
 
         def store_v(c):
             v_out = out_pool.tile([P, TILES * HEAD], F32, name="v_out")
             nc.scalar.copy(out=v_out[:], in_=head_tiles[c, "v"][:])
             nc.sync.dma_start(out=v_chunks[c], in_=v_out[:])
 
-        def multiply(c):
+        def multiply_q(c):
             products = out_pool.tile([P, 2, ROT_VECTORS, HEAD], F32, name="products")
             first = (c % SEQ_CHUNKS) * TILES
             vectors = Q_BANK_TILES * Q_HEADS
@@ -135,8 +142,12 @@ def tile_attention_pa_t_kernel(tc, x, cos, sin, Wq, Wk, Wv, out_0, out_1, out_2)
                     in1=tables[:, :, tile0 : tile0 + Q_BANK_TILES, :, :].rearrange("p w j h d -> p w (j h d)"),
                     op=ALU.mult,
                 )
+            product_tiles[c] = products
+
+        def multiply_k(c):
+            first = (c % SEQ_CHUNKS) * TILES
             nc.vector.tensor_tensor(
-                out=products[:, :, Q_VECTORS:ROT_VECTORS, :],
+                out=product_tiles[c][:, :, Q_VECTORS:ROT_VECTORS, :],
                 in0=head_tiles[c, "k"][:]
                 .rearrange("p (j d) -> p j d", d=HEAD)
                 .unsqueeze(1)
@@ -144,7 +155,6 @@ def tile_attention_pa_t_kernel(tc, x, cos, sin, Wq, Wk, Wv, out_0, out_1, out_2)
                 in1=tables[:, :, first : first + TILES, 0, :],
                 op=ALU.mult,
             )
-            product_tiles[c] = products
 
         def add(c):
             adder = nc.gpsimd if c < CHUNKS - 1 else nc.vector
@@ -165,50 +175,19 @@ def tile_attention_pa_t_kernel(tc, x, cos, sin, Wq, Wk, Wv, out_0, out_1, out_2)
         ident = const.tile([P, P], F32)
         make_identity(nc, ident[:])
 
-        w_raws = []
-        for name, w in (("wq_raw", Wq), ("wk_raw", Wk), ("wv_raw", Wv)):
-            w_raw = const.tile([P, PASSES, PACK, w.shape[1]], BF16, name=name)
-            nc.sync.dma_start(
-                out=w_raw[:].rearrange("p g t n -> p g (t n)"),
-                in_=w.rearrange("(g q t) n -> q g (t n)", q=P, t=PACK),
-            )
-            w_raws.append((w_raw, w.shape[1]))
-
-        load(0, pieces=TILES)
-
         sin_sb = const.tile([P, SEQ_CHUNKS * TILES, HEAD], BF16)
         cos_sb = const.tile([P, SEQ_CHUNKS * TILES, HEAD], BF16)
-        for table_sb, table in ((sin_sb, sin), (cos_sb, cos)):
-            nc.sync.dma_start(
-                out=table_sb[:].rearrange("p (c j) d -> p c (j d)", j=TILES),
-                in_=table.rearrange("(c p j) d -> p c (j d)", p=P, j=TILES),
-            )
 
-        for c in range(1, LOAD_AHEAD):
-            load(c)
-
-        w_grouped = const.tile([P, PASSES, OUT_COLS, PACK], BF16, align_bytes=64)
-        w_first = 0
-        for w_raw, w_cols in w_raws:
-            for g in range(PASSES):
-                nc.vector.tensor_copy(
-                    out=w_grouped[:, g, w_first : w_first + w_cols, :],
-                    in_=w_raw[:, g].rearrange("p t n -> p n t"),
+        def load_tables(first, end):
+            for table_sb, table in ((sin_sb, sin), (cos_sb, cos)):
+                nc.sync.dma_start(
+                    out=table_sb[:, first * TILES : end * TILES, :].rearrange("p (c j) d -> p c (j d)", j=TILES),
+                    in_=table.rearrange("(c p j) d -> p c (j d)", p=P, j=TILES)[:, first:end],
                 )
-            w_first += w_cols
-        w_codes = const.tile([P, PASSES * OUT_COLS], U32, align_bytes=64)
-        w_scales = const.tile([P, PASSES * OUT_COLS], U8, align_bytes=64)
-        nc.vector.quantize_mx(
-            out=w_codes[:].bitcast(FP8X4),
-            scales=w_scales[:],
-            in_=w_grouped[:].rearrange("p g n t -> p (g n t)"),
-        )
-
-        transpose(0)
-        transpose(1)
 
         tables = const.tile([P, 2, SEQ_CHUNKS * TILES, Q_HEADS, HEAD], BF16)
-        for c in range(SEQ_CHUNKS):
+
+        def build_tables(c):
             rows = slice(c * TILES, (c + 1) * TILES)
             cos_rows = cos_sb[:, rows, :].unsqueeze(2).to_broadcast([P, TILES, Q_HEADS, HEAD])
             sin_rows = sin_sb[:, rows, :].unsqueeze(2).to_broadcast([P, TILES, Q_HEADS, HEAD])
@@ -216,19 +195,69 @@ def tile_attention_pa_t_kernel(tc, x, cos, sin, Wq, Wk, Wv, out_0, out_1, out_2)
             nc.scalar.copy(out=tables[:, 1, rows, :, 0:HALF], in_=sin_rows[:, :, :, HALF:HEAD])
             nc.scalar.mul(tables[:, 1, rows, :, HALF:HEAD], sin_rows[:, :, :, 0:HALF], -1.0)
 
-        quantise(0)
+        w_raws = {}
+
+        def load_weight(name, w):
+            w_raw = const.tile([P, PASSES, PACK, w.shape[1]], BF16, name=name + "_raw")
+            nc.sync.dma_start(
+                out=w_raw[:].rearrange("p g t n -> p g (t n)"),
+                in_=w.rearrange("(g q t) n -> q g (t n)", q=P, t=PACK),
+            )
+            w_raws[name] = w_raw
+
+        def quantise_weight(name):
+            w_raw = w_raws[name]
+            cols = w_raw.shape[3]
+            w_grouped = const.tile([P, PASSES, cols, PACK], BF16, name=name + "_grouped", align_bytes=64)
+            for g in range(PASSES):
+                nc.vector.tensor_copy(out=w_grouped[:, g], in_=w_raw[:, g].rearrange("p t n -> p n t"))
+            w_codes = const.tile([P, PASSES * cols], U32, name=name + "_codes", align_bytes=64)
+            w_scales = const.tile([P, PASSES * cols], U8, name=name + "_scales", align_bytes=64)
+            nc.vector.quantize_mx(
+                out=w_codes[:].bitcast(FP8X4),
+                scales=w_scales[:],
+                in_=w_grouped[:].rearrange("p g n t -> p (g n t)"),
+            )
+            w_operands[name] = (w_codes, w_scales, cols)
+
+        load_weight("q", Wq)
+        load(0, pieces=TILES)
+        load_weight("k", Wk)
+        load_weight("v", Wv)
+        load_tables(0, 1)
+        load(1)
+        load_tables(1, SEQ_CHUNKS)
+        for c in range(2, LOAD_AHEAD):
+            load(c)
+
+        transpose(0)
+        quantise_weight("q")
+        quantise(0, pieces=2)
+        quantise_weight("k")
+        quantise_weight("v")
+        build_tables(0)
+
         for c in range(CHUNKS):
             if c + LOAD_AHEAD < CHUNKS:
                 load(c + LOAD_AHEAD)
-            if c + 1 < CHUNKS:
-                quantise(c + 1)
-            project_q(c)
-            project_kv(c)
-            store_v(c)
+            if c == 0:
+                project_q(0)
+                transpose(1)
+                multiply_q(0)
+                quantise(1)
+            else:
+                if c + 1 < CHUNKS:
+                    quantise(c + 1)
+                project_q(c)
+                multiply_q(c)
             if c + 2 < CHUNKS:
                 transpose(c + 2)
-            multiply(c)
+            project_kv(c)
+            store_v(c)
+            multiply_k(c)
             add(c)
+            if c + 1 < SEQ_CHUNKS:
+                build_tables(c + 1)
             if c > 0:
                 store_qk(c - 1)
         store_qk(CHUNKS - 1)

@@ -26,6 +26,7 @@ PAIR = 2
 TILES = 4
 Q_BANK_TILES = 2
 Q_BANKS = TILES // Q_BANK_TILES
+BANK_TILES = [range(b * Q_BANK_TILES, (b + 1) * Q_BANK_TILES) for b in range(Q_BANKS)]
 CHUNKS = BATCH * SEQ // (TILES * P)
 SEQ_CHUNKS = SEQ // (TILES * P)
 Q_VECTORS = TILES * Q_HEADS
@@ -58,21 +59,20 @@ def tile_attention_pa_t_kernel(tc, x, cos, sin, Wq, Wk, Wv, out_0, out_1, out_2)
         x_tiles, grouped_tiles, code_tiles, scale_tiles, head_tiles, product_tiles = {}, {}, {}, {}, {}, {}
         w_operands = {}
 
-        def load(c, pieces=1):
-            x_sb = x_pool.tile([P, TILES * HID], BF16, name="x_sb")
-            width = TILES * HID // pieces
-            for i in range(pieces):
-                columns = slice(i * width, (i + 1) * width)
-                nc.sync.dma_start(out=x_sb[:, columns], in_=x_chunks[c][:, columns])
-            x_tiles[c] = x_sb
+        def load(c, tiles=range(TILES)):
+            if tiles[0] == 0:
+                x_tiles[c] = x_pool.tile([P, TILES * HID], BF16, name="x_sb")
+            columns = slice(tiles[0] * HID, (tiles[-1] + 1) * HID)
+            nc.sync.dma_start(out=x_tiles[c][:, columns], in_=x_chunks[c][:, columns])
 
-        def transpose(c):
+        def transpose(c, tiles=range(TILES)):
             x_words = x_tiles[c][:].bitcast(F32)
-            grouped = mx_pool.tile([P, TILES * HID], BF16, name="grouped", align_bytes=64)
-            grouped_words = grouped[:].bitcast(F32).rearrange(
+            if tiles[0] == 0:
+                grouped_tiles[c] = mx_pool.tile([P, TILES * HID], BF16, name="grouped", align_bytes=64)
+            grouped_words = grouped_tiles[c][:].bitcast(F32).rearrange(
                 "p (j g r u) -> p j g r u", j=TILES, g=PASSES, u=PAIR
             )
-            for j in range(TILES):
+            for j in tiles:
                 xt = xt_psum.tile([P, PASSES, PAIR, P], F32, name="xt")
                 for g in range(PASSES):
                     for u in range(PAIR):
@@ -83,20 +83,18 @@ def tile_attention_pa_t_kernel(tc, x, cos, sin, Wq, Wk, Wv, out_0, out_1, out_2)
                             identity=ident[:],
                         )
                 nc.scalar.copy(out=grouped_words[:, j], in_=xt[:].rearrange("p g u r -> p g r u"))
-            grouped_tiles[c] = grouped
 
-        def quantise(c, pieces=1):
-            x_codes = mx_pool.tile([P, TILES * PASSES * P], U32, name="x_codes", align_bytes=64)
-            x_scales = mx_pool.tile([P, TILES * PASSES * P], U8, name="x_scales", align_bytes=64)
-            words = TILES * PASSES * P // pieces
-            for i in range(pieces):
-                columns = slice(i * words, (i + 1) * words)
-                nc.vector.quantize_mx(
-                    out=x_codes[:, columns].bitcast(FP8X4),
-                    scales=x_scales[:, columns],
-                    in_=grouped_tiles[c][:, i * words * PACK : (i + 1) * words * PACK],
-                )
-            code_tiles[c], scale_tiles[c] = x_codes, x_scales
+        def quantise(c, tiles=range(TILES)):
+            if tiles[0] == 0:
+                words = TILES * PASSES * P
+                code_tiles[c] = mx_pool.tile([P, words], U32, name="x_codes", align_bytes=64)
+                scale_tiles[c] = mx_pool.tile([P, words], U8, name="x_scales", align_bytes=64)
+            first, end = tiles[0] * PASSES * P, (tiles[-1] + 1) * PASSES * P
+            nc.vector.quantize_mx(
+                out=code_tiles[c][:, first:end].bitcast(FP8X4),
+                scales=scale_tiles[c][:, first:end],
+                in_=grouped_tiles[c][:, first * PACK : end * PACK],
+            )
 
         def project(c, name, tiles, weight):
             w_codes, w_scales, cols = w_operands[weight]
@@ -116,148 +114,206 @@ def tile_attention_pa_t_kernel(tc, x, cos, sin, Wq, Wk, Wv, out_0, out_1, out_2)
                     )
             head_tiles[c, name] = acc
 
-        def project_q(c):
-            for b in range(Q_BANKS):
-                tiles = range(b * Q_BANK_TILES, (b + 1) * Q_BANK_TILES)
-                project(c, "q%d" % b, tiles, "q")
+        def project_q(c, b):
+            project(c, "q%d" % b, BANK_TILES[b], "q")
 
-        def project_kv(c):
-            for name in ("k", "v"):
-                project(c, name, range(TILES), name)
+        def project_k(c):
+            project(c, "k", range(TILES), "k")
+
+        def project_v(c):
+            project(c, "v", range(TILES), "v")
 
         def store_v(c):
             v_out = out_pool.tile([P, TILES * HEAD], F32, name="v_out")
             nc.scalar.copy(out=v_out[:], in_=head_tiles[c, "v"][:])
             nc.sync.dma_start(out=v_chunks[c], in_=v_out[:])
 
-        def multiply_q(c):
-            products = out_pool.tile([P, 2, ROT_VECTORS, HEAD], F32, name="products")
-            first = (c % SEQ_CHUNKS) * TILES
+        def multiply_q(c, b):
+            if b == 0:
+                product_tiles[c] = out_pool.tile([P, 2, ROT_VECTORS, HEAD], F32, name="products")
             vectors = Q_BANK_TILES * Q_HEADS
-            for b in range(Q_BANKS):
-                tile0 = first + b * Q_BANK_TILES
-                nc.vector.tensor_tensor(
-                    out=products[:, :, b * vectors : (b + 1) * vectors, :].rearrange("p w n d -> p w (n d)"),
-                    in0=head_tiles[c, "q%d" % b][:].unsqueeze(1).to_broadcast([P, 2, vectors * HEAD]),
-                    in1=tables[:, :, tile0 : tile0 + Q_BANK_TILES, :, :].rearrange("p w j h d -> p w (j h d)"),
-                    op=ALU.mult,
-                )
-            product_tiles[c] = products
-
-        def multiply_k(c):
-            first = (c % SEQ_CHUNKS) * TILES
+            shape = [P, 2, Q_BANK_TILES, Q_HEADS, HEAD]
             nc.vector.tensor_tensor(
-                out=product_tiles[c][:, :, Q_VECTORS:ROT_VECTORS, :],
-                in0=head_tiles[c, "k"][:]
-                .rearrange("p (j d) -> p j d", d=HEAD)
+                out=product_tiles[c][:, :, b * vectors : (b + 1) * vectors, :].rearrange(
+                    "p w (j h) d -> p w j h d", h=Q_HEADS
+                ),
+                in0=head_tiles[c, "q%d" % b][:]
+                .rearrange("p (j h d) -> p j h d", h=Q_HEADS, d=HEAD)
                 .unsqueeze(1)
-                .to_broadcast([P, 2, TILES, HEAD]),
-                in1=tables[:, :, first : first + TILES, 0, :],
+                .to_broadcast(shape),
+                in1=tables[:, (c % SEQ_CHUNKS) * Q_BANKS + b]
+                .rearrange("p w (j d) -> p w j d", d=HEAD)
+                .unsqueeze(3)
+                .to_broadcast(shape),
                 op=ALU.mult,
             )
 
-        def add(c):
-            adder = nc.gpsimd if c < CHUNKS - 1 else nc.vector
-            rot = product_tiles[c][:, 0]
-            rot_halves = rot.rearrange("p n (f d) -> p n f d", f=2)
-            cross_halves = product_tiles[c][:, 1].rearrange("p n (f d) -> p n f d", f=2)
-            adder.tensor_tensor(
-                out=rot_halves, in0=rot_halves, in1=cross_halves[:, :, ::-1, :], op=ALU.add
+        def multiply_k(c):
+            first = (c % SEQ_CHUNKS) * Q_BANKS
+            shape = [P, 2, Q_BANKS, Q_BANK_TILES * HEAD]
+            nc.vector.tensor_tensor(
+                out=product_tiles[c][:, :, Q_VECTORS:ROT_VECTORS, :].rearrange(
+                    "p w (b j) d -> p w b (j d)", b=Q_BANKS
+                ),
+                in0=head_tiles[c, "k"][:].rearrange("p (b n) -> p b n", b=Q_BANKS).unsqueeze(1).to_broadcast(shape),
+                in1=tables[:, first : first + Q_BANKS].rearrange("p b w n -> p w b n"),
+                op=ALU.mult,
             )
 
-        def store_qk(c):
-            rot = product_tiles[c][:, 0]
-            nc.sync.dma_start(out=q_chunks[c], in_=rot[:, 0:Q_VECTORS, :].rearrange("p n d -> p (n d)"))
+        def add(c, engine, first, end):
+            vectors = product_tiles[c][:, :, first:end, :].rearrange("p w n (f d) -> p w n f d", f=2)
+            rot, cross = vectors[:, 0], vectors[:, 1]
+            engine.tensor_tensor(out=rot, in0=rot, in1=cross[:, :, ::-1, :], op=ALU.add)
+
+        def store_q(c, first=0, end=Q_VECTORS):
+            rot = product_tiles[c][:, 0, first:end, :]
             nc.sync.dma_start(
-                out=k_chunks[c], in_=rot[:, Q_VECTORS:ROT_VECTORS, :].rearrange("p n d -> p (n d)")
+                out=q_chunks[c][:, first * HEAD : end * HEAD], in_=rot.rearrange("p n d -> p (n d)")
             )
+
+        def store_k(c):
+            rot = product_tiles[c][:, 0, Q_VECTORS:ROT_VECTORS, :]
+            nc.sync.dma_start(out=k_chunks[c], in_=rot.rearrange("p n d -> p (n d)"))
 
         ident = const.tile([P, P], F32)
         make_identity(nc, ident[:])
 
-        sin_sb = const.tile([P, SEQ_CHUNKS * TILES, HEAD], BF16)
-        cos_sb = const.tile([P, SEQ_CHUNKS * TILES, HEAD], BF16)
+        table_rows = Q_BANK_TILES * HEAD
+        tables = const.tile([P, SEQ_CHUNKS * Q_BANKS, 2, table_rows], BF16)
+        sin_sb = const.tile([P, SEQ_CHUNKS * Q_BANKS, table_rows], BF16)
 
         def load_tables(first, end):
-            for table_sb, table in ((sin_sb, sin), (cos_sb, cos)):
-                nc.sync.dma_start(
-                    out=table_sb[:, first * TILES : end * TILES, :].rearrange("p (c j) d -> p c (j d)", j=TILES),
-                    in_=table.rearrange("(c p j) d -> p c (j d)", p=P, j=TILES)[:, first:end],
-                )
-
-        tables = const.tile([P, 2, SEQ_CHUNKS * TILES, Q_HEADS, HEAD], BF16)
+            banks = slice(first * Q_BANKS, end * Q_BANKS)
+            for table_sb, table in ((sin_sb[:, banks], sin), (tables[:, banks, 0], cos)):
+                by_bank = table.rearrange("(c p b j) d -> p c b (j d)", p=P, b=Q_BANKS, j=Q_BANK_TILES)
+                for c in range(first, end):
+                    b = (c - first) * Q_BANKS
+                    nc.sync.dma_start(out=table_sb[:, b : b + Q_BANKS], in_=by_bank[:, c])
 
         def build_tables(c):
-            rows = slice(c * TILES, (c + 1) * TILES)
-            cos_rows = cos_sb[:, rows, :].unsqueeze(2).to_broadcast([P, TILES, Q_HEADS, HEAD])
-            sin_rows = sin_sb[:, rows, :].unsqueeze(2).to_broadcast([P, TILES, Q_HEADS, HEAD])
-            nc.scalar.copy(out=tables[:, 0, rows, :, :], in_=cos_rows)
-            nc.scalar.copy(out=tables[:, 1, rows, :, 0:HALF], in_=sin_rows[:, :, :, HALF:HEAD])
-            nc.scalar.mul(tables[:, 1, rows, :, HALF:HEAD], sin_rows[:, :, :, 0:HALF], -1.0)
+            banks = slice(c * Q_BANKS, (c + 1) * Q_BANKS)
+            swapped = tables[:, banks, 1].rearrange("p b (j d) -> p b j d", d=HEAD)
+            rows = sin_sb[:, banks].rearrange("p b (j d) -> p b j d", d=HEAD)
+            nc.scalar.copy(out=swapped[:, :, :, 0:HALF], in_=rows[:, :, :, HALF:HEAD])
+            nc.scalar.mul(swapped[:, :, :, HALF:HEAD], rows[:, :, :, 0:HALF], -1.0)
 
-        w_raws = {}
+        w_raws, w_groups = {}, {}
 
-        def load_weight(name, w):
-            w_raw = const.tile([P, PASSES, PACK, w.shape[1]], BF16, name=name + "_raw")
+        def load_weight(name, w, passes=range(PASSES)):
+            if passes[0] == 0:
+                w_raws[name] = const.tile([P, PASSES, PACK, w.shape[1]], BF16, name=name + "_raw")
+            passes = slice(passes[0], passes[-1] + 1)
             nc.sync.dma_start(
-                out=w_raw[:].rearrange("p g t n -> p g (t n)"),
-                in_=w.rearrange("(g q t) n -> q g (t n)", q=P, t=PACK),
+                out=w_raws[name][:, passes].rearrange("p g t n -> p g (t n)"),
+                in_=w.rearrange("(g q t) n -> q g (t n)", q=P, t=PACK)[:, passes],
             )
-            w_raws[name] = w_raw
+
+        def group_weight(name):
+            w_raw = w_raws[name]
+            shape = [P, PASSES, w_raw.shape[3], PACK]
+            w_groups[name] = const.tile(shape, BF16, name=name + "_grouped", align_bytes=64)
+            for g in range(PASSES):
+                nc.vector.tensor_copy(out=w_groups[name][:, g], in_=w_raw[:, g].rearrange("p t n -> p n t"))
 
         def quantise_weight(name):
-            w_raw = w_raws[name]
-            cols = w_raw.shape[3]
-            w_grouped = const.tile([P, PASSES, cols, PACK], BF16, name=name + "_grouped", align_bytes=64)
-            for g in range(PASSES):
-                nc.vector.tensor_copy(out=w_grouped[:, g], in_=w_raw[:, g].rearrange("p t n -> p n t"))
+            cols = w_raws[name].shape[3]
             w_codes = const.tile([P, PASSES * cols], U32, name=name + "_codes", align_bytes=64)
             w_scales = const.tile([P, PASSES * cols], U8, name=name + "_scales", align_bytes=64)
             nc.vector.quantize_mx(
                 out=w_codes[:].bitcast(FP8X4),
                 scales=w_scales[:],
-                in_=w_grouped[:].rearrange("p g n t -> p (g n t)"),
+                in_=w_groups[name][:].rearrange("p g n t -> p (g n t)"),
             )
             w_operands[name] = (w_codes, w_scales, cols)
 
-        load_weight("q", Wq)
-        load(0, pieces=TILES)
+        early, late = BANK_TILES
+        load_weight("q", Wq, range(0, 1))
+        load(0, range(0, 1))
+        load(0, range(1, 2))
+        load_weight("q", Wq, range(1, 2))
+        load(0, range(2, 3))
+        load(0, range(3, 4))
         load_weight("k", Wk)
-        load_weight("v", Wv)
         load_tables(0, 1)
-        load(1)
-        load_tables(1, SEQ_CHUNKS)
-        for c in range(2, LOAD_AHEAD):
-            load(c)
+        load(1, early)
+        load_weight("v", Wv)
+        load(1, late)
+        load_tables(1, 2)
+        load(2)
+        load(3)
+        load_tables(2, SEQ_CHUNKS)
+        load(4)
+        load(5)
 
         transpose(0)
-        quantise_weight("q")
-        quantise(0, pieces=2)
-        quantise_weight("k")
-        quantise_weight("v")
         build_tables(0)
+        group_weight("q")
+        quantise_weight("q")
+        quantise(0, early)
+        group_weight("k")
+        project_q(0, 0)
+        quantise_weight("k")
+        multiply_q(0, 0)
+        quantise(0, late)
+        group_weight("v")
+        quantise_weight("v")
 
-        for c in range(CHUNKS):
+        transpose(1, early)
+        project_q(0, 1)
+        multiply_q(0, 1)
+        transpose(1, late)
+        quantise(1, early)
+        project_k(0)
+        multiply_k(0)
+        gpsimd_vectors = Q_VECTORS + 1
+        add(0, nc.gpsimd, 0, gpsimd_vectors)
+        quantise(1, late)
+        build_tables(1)
+        transpose(2, early)
+        project_q(1, 0)
+        multiply_q(1, 0)
+        transpose(2, late)
+        project_q(1, 1)
+        multiply_q(1, 1)
+        project_k(1)
+        project_v(0)
+        store_v(0)
+        quantise(2)
+        add(0, nc.vector, gpsimd_vectors, ROT_VECTORS)
+        store_q(0)
+        store_k(0)
+        multiply_k(1)
+        add(1, nc.gpsimd, 0, ROT_VECTORS)
+        transpose(3)
+        project_v(1)
+        store_v(1)
+        build_tables(2)
+
+        for c in range(2, CHUNKS):
             if c + LOAD_AHEAD < CHUNKS:
                 load(c + LOAD_AHEAD)
-            if c == 0:
-                project_q(0)
-                transpose(1)
-                multiply_q(0)
-                quantise(1)
-            else:
-                if c + 1 < CHUNKS:
-                    quantise(c + 1)
-                project_q(c)
-                multiply_q(c)
+            if c + 1 < CHUNKS:
+                quantise(c + 1)
+            for b in range(Q_BANKS):
+                project_q(c, b)
+                multiply_q(c, b)
             if c + 2 < CHUNKS:
                 transpose(c + 2)
-            project_kv(c)
+            project_k(c)
+            project_v(c)
             store_v(c)
             multiply_k(c)
-            add(c)
+            if c < CHUNKS - 1:
+                add(c, nc.gpsimd, 0, ROT_VECTORS)
             if c + 1 < SEQ_CHUNKS:
                 build_tables(c + 1)
-            if c > 0:
-                store_qk(c - 1)
-        store_qk(CHUNKS - 1)
+            store_q(c - 1)
+            store_k(c - 1)
+
+        last = CHUNKS - 1
+        half = Q_VECTORS // 2
+        for first in (0, half):
+            add(last, nc.vector, first, first + half)
+            store_q(last, first, first + half)
+        add(last, nc.vector, Q_VECTORS, ROT_VECTORS)
+        store_k(last)

@@ -51,13 +51,13 @@ def tile_attention_pa_t_kernel(tc, x, cos, sin, Wq, Wk, Wv, out_0, out_1, out_2)
         stack.enter_context(tc.manual_schedule())
         const = stack.enter_context(tc.tile_pool(name="const", bufs=1))
         x_pool = stack.enter_context(tc.tile_pool(name="x", bufs=X_BUFS))
-        mx_pool = stack.enter_context(tc.tile_pool(name="mx", bufs=2))
+        mx_pool = stack.enter_context(tc.tile_pool(name="mx", bufs=3))
         out_pool = stack.enter_context(tc.tile_pool(name="out", bufs=3))
         xt_psum = stack.enter_context(tc.psum_pool(name="xt_psum", bufs=TILES))
         head_psum = stack.enter_context(tc.psum_pool(name="head_psum", bufs=1))
 
         x_tiles, grouped_tiles, code_tiles, scale_tiles, head_tiles, product_tiles = {}, {}, {}, {}, {}, {}
-        w_operands = {}
+        rot_tiles, w_operands = {}, {}
 
         def load(c, tiles=range(TILES)):
             if tiles[0] == 0:
@@ -161,18 +161,24 @@ def tile_attention_pa_t_kernel(tc, x, cos, sin, Wq, Wk, Wv, out_0, out_1, out_2)
             )
 
         def add(c, engine, first, end):
+            if first == 0:
+                rot_tiles[c] = out_pool.tile([P, ROT_VECTORS, HEAD], F32, name="rot")
             vectors = product_tiles[c][:, :, first:end, :].rearrange("p w n (f d) -> p w n f d", f=2)
-            rot, cross = vectors[:, 0], vectors[:, 1]
-            engine.tensor_tensor(out=rot, in0=rot, in1=cross[:, :, ::-1, :], op=ALU.add)
+            engine.tensor_tensor(
+                out=rot_tiles[c][:, first:end, :].rearrange("p n (f d) -> p n f d", f=2),
+                in0=vectors[:, 0],
+                in1=vectors[:, 1, :, ::-1, :],
+                op=ALU.add,
+            )
 
         def store_q(c, first=0, end=Q_VECTORS):
-            rot = product_tiles[c][:, 0, first:end, :]
+            rot = rot_tiles[c][:, first:end, :]
             nc.sync.dma_start(
                 out=q_chunks[c][:, first * HEAD : end * HEAD], in_=rot.rearrange("p n d -> p (n d)")
             )
 
         def store_k(c):
-            rot = product_tiles[c][:, 0, Q_VECTORS:ROT_VECTORS, :]
+            rot = rot_tiles[c][:, Q_VECTORS:ROT_VECTORS, :]
             nc.sync.dma_start(out=k_chunks[c], in_=rot.rearrange("p n d -> p (n d)"))
 
         ident = const.tile([P, P], F32)

@@ -281,18 +281,16 @@ def tile_attention_pa_t_kernel(tc, x, cos, sin, Wq, Wk, Wv, out_0, out_1, out_2)
         transpose(2, late)
         project_q(1, 1)
         multiply_q(1, 1)
-        project_k(1)
-        project_v(0)
-        store_v(0)
         quantise(2)
         add(0, nc.vector, gpsimd_vectors, ROT_VECTORS)
         store_q(0)
         store_k(0)
+        transpose(3)
+        project_k(1)
         multiply_k(1)
         add(1, nc.gpsimd, 0, ROT_VECTORS)
-        transpose(3)
-        project_v(1)
-        store_v(1)
+        project_v(0)
+        store_v(0)
         build_tables(2)
 
         for c in range(2, CHUNKS):
@@ -303,18 +301,24 @@ def tile_attention_pa_t_kernel(tc, x, cos, sin, Wq, Wk, Wv, out_0, out_1, out_2)
             for b in range(Q_BANKS):
                 project_q(c, b)
                 multiply_q(c, b)
+            if c == 2:
+                project_v(1)
+                store_v(1)
             if c + 2 < CHUNKS:
                 transpose(c + 2)
+            store_q(c - 1)
             project_k(c)
             project_v(c)
             store_v(c)
+            store_k(c - 1)
             multiply_k(c)
-            if c < CHUNKS - 1:
+            if c < CHUNKS - 2:
                 add(c, nc.gpsimd, 0, ROT_VECTORS)
+            elif c == CHUNKS - 2:
+                add(c, nc.gpsimd, 0, Q_VECTORS)
+                add(c, nc.gpsimd, Q_VECTORS, ROT_VECTORS)
             if c + 1 < SEQ_CHUNKS:
                 build_tables(c + 1)
-            store_q(c - 1)
-            store_k(c - 1)
 
         last = CHUNKS - 1
         half = Q_VECTORS // 2

@@ -34,6 +34,8 @@ ROT_VECTORS = TILES * ROT_HEADS
 
 LOAD_AHEAD = 4
 X_BUFS = LOAD_AHEAD + 2
+SORT_AHEAD = 3
+SORTED_TILES = (3,)
 
 FLOPS = 2 * BATCH * SEQ * HID * OUT_COLS
 
@@ -51,19 +53,28 @@ def tile_attention_pa_t_kernel(tc, x, cos, sin, Wq, Wk, Wv, out_0, out_1, out_2)
         stack.enter_context(tc.manual_schedule())
         const = stack.enter_context(tc.tile_pool(name="const", bufs=1))
         x_pool = stack.enter_context(tc.tile_pool(name="x", bufs=X_BUFS))
+        sort_pool = stack.enter_context(tc.tile_pool(name="sort", bufs=2))
         mx_pool = stack.enter_context(tc.tile_pool(name="mx", bufs=3))
         out_pool = stack.enter_context(tc.tile_pool(name="out", bufs=3))
         xt_psum = stack.enter_context(tc.psum_pool(name="xt_psum", bufs=TILES))
         head_psum = stack.enter_context(tc.psum_pool(name="head_psum", bufs=1))
 
         x_tiles, grouped_tiles, code_tiles, scale_tiles, head_tiles, product_tiles = {}, {}, {}, {}, {}, {}
-        rot_tiles, w_operands = {}, {}
+        rot_tiles, w_operands, sorted_tiles = {}, {}, {}
 
         def load(c, tiles=range(TILES)):
             if tiles[0] == 0:
                 x_tiles[c] = x_pool.tile([P, TILES * HID], BF16, name="x_sb")
             columns = slice(tiles[0] * HID, (tiles[-1] + 1) * HID)
             nc.sync.dma_start(out=x_tiles[c][:, columns], in_=x_chunks[c][:, columns])
+
+        def sort(c):
+            sorted_tiles[c] = sort_pool.tile([P, len(SORTED_TILES), PASSES, PAIR, P], F32, name="x_sorted")
+            x_words = x_tiles[c][:].bitcast(F32).rearrange(
+                "p (j g r u) -> p j g u r", j=TILES, g=PASSES, u=PAIR
+            )
+            for i, j in enumerate(SORTED_TILES):
+                nc.scalar.copy(out=sorted_tiles[c][:, i], in_=x_words[:, j])
 
         def transpose(c, tiles=range(TILES)):
             x_words = x_tiles[c][:].bitcast(F32)
@@ -77,11 +88,11 @@ def tile_attention_pa_t_kernel(tc, x, cos, sin, Wq, Wk, Wv, out_0, out_1, out_2)
                 for g in range(PASSES):
                     for u in range(PAIR):
                         first = (j * PASSES + g) * PAIR * P
-                        nc.tensor.transpose(
-                            out=xt[:, g, u, :],
-                            in_=x_words[:, first + u : first + PAIR * P : PAIR],
-                            identity=ident[:],
-                        )
+                        if c in sorted_tiles and j in SORTED_TILES:
+                            words = sorted_tiles[c][:, SORTED_TILES.index(j), g, u, :]
+                        else:
+                            words = x_words[:, first + u : first + PAIR * P : PAIR]
+                        nc.tensor.transpose(out=xt[:, g, u, :], in_=words, identity=ident[:])
                 nc.scalar.copy(out=grouped_words[:, j], in_=xt[:].rearrange("p g u r -> p g r u"))
 
         def quantise(c, tiles=range(TILES)):
@@ -306,6 +317,8 @@ def tile_attention_pa_t_kernel(tc, x, cos, sin, Wq, Wk, Wv, out_0, out_1, out_2)
                 store_v(1)
             if c + 2 < CHUNKS:
                 transpose(c + 2)
+            if c + SORT_AHEAD < CHUNKS:
+                sort(c + SORT_AHEAD)
             store_q(c - 1)
             project_k(c)
             project_v(c)

from contextlib import ExitStack

import concourse.mybir as mybir
from concourse.masks import make_identity

F32 = mybir.dt.float32
BF16 = mybir.dt.bfloat16
U32 = mybir.dt.uint32
U8 = mybir.dt.uint8
FP8X4 = mybir.dt.float8_e4m3fn_x4
ALU = mybir.AluOpType

P = 128
BATCH, SEQ, HID = 4, 2048, 1024
HEAD = 128
HALF = HEAD // 2
Q_HEADS = 2
ROT_HEADS = Q_HEADS + 1
HEADS = ROT_HEADS + 1
OUT_COLS = HEADS * HEAD

PACK = 4
PASSES = HID // (P * PACK)
PAIR = 2

TILES = 4
Q_BANK_TILES = 2
Q_BANKS = TILES // Q_BANK_TILES
BANK_TILES = [range(b * Q_BANK_TILES, (b + 1) * Q_BANK_TILES) for b in range(Q_BANKS)]
CHUNKS = BATCH * SEQ // (TILES * P)
SEQ_CHUNKS = SEQ // (TILES * P)
Q_VECTORS = TILES * Q_HEADS
ROT_VECTORS = TILES * ROT_HEADS

LOAD_AHEAD = 4
X_BUFS = LOAD_AHEAD + 2
SORT_AHEAD = 3
SORTED_TILES = (3,)

FLOPS = 2 * BATCH * SEQ * HID * OUT_COLS


def tile_attention_pa_t_kernel(tc, x, cos, sin, Wq, Wk, Wv, out_0, out_1, out_2):
    nc = tc.nc

    by_chunk = "(c p j) n -> c p (j n)"
    x_chunks = x.flatten_outer_dims().rearrange(by_chunk, p=P, j=TILES)
    q_chunks = out_0.rearrange("b s h d -> (b s) (h d)").rearrange(by_chunk, p=P, j=TILES)
    k_chunks = out_1.rearrange("b s h d -> (b s) (h d)").rearrange(by_chunk, p=P, j=TILES)
    v_chunks = out_2.rearrange("b s h d -> (b s) (h d)").rearrange(by_chunk, p=P, j=TILES)

    with ExitStack() as stack:
        stack.enter_context(tc.manual_schedule())
        const = stack.enter_context(tc.tile_pool(name="const", bufs=1))
        x_pool = stack.enter_context(tc.tile_pool(name="x", bufs=X_BUFS))
        sort_pool = stack.enter_context(tc.tile_pool(name="sort", bufs=2))
        mx_pool = stack.enter_context(tc.tile_pool(name="mx", bufs=3))
        out_pool = stack.enter_context(tc.tile_pool(name="out", bufs=3))
        xt_psum = stack.enter_context(tc.psum_pool(name="xt_psum", bufs=TILES))
        head_psum = stack.enter_context(tc.psum_pool(name="head_psum", bufs=1))

        x_tiles, grouped_tiles, code_tiles, scale_tiles, head_tiles, product_tiles = {}, {}, {}, {}, {}, {}
        rot_tiles, w_operands, sorted_tiles = {}, {}, {}

        def load(c, tiles=range(TILES)):
            if tiles[0] == 0:
                x_tiles[c] = x_pool.tile([P, TILES * HID], BF16, name="x_sb")
            columns = slice(tiles[0] * HID, (tiles[-1] + 1) * HID)
            nc.sync.dma_start(out=x_tiles[c][:, columns], in_=x_chunks[c][:, columns])

        def sort(c):
            sorted_tiles[c] = sort_pool.tile([P, len(SORTED_TILES), PASSES, PAIR, P], F32, name="x_sorted")
            x_words = x_tiles[c][:].bitcast(F32).rearrange(
                "p (j g r u) -> p j g u r", j=TILES, g=PASSES, u=PAIR
            )
            for i, j in enumerate(SORTED_TILES):
                nc.scalar.copy(out=sorted_tiles[c][:, i], in_=x_words[:, j])

        def transpose(c, tiles=range(TILES)):
            x_words = x_tiles[c][:].bitcast(F32)
            if tiles[0] == 0:
                grouped_tiles[c] = mx_pool.tile([P, TILES * HID], BF16, name="grouped", align_bytes=64)
            grouped_words = grouped_tiles[c][:].bitcast(F32).rearrange(
                "p (j g r u) -> p j g r u", j=TILES, g=PASSES, u=PAIR
            )
            for j in tiles:
                xt = xt_psum.tile([P, PASSES, PAIR, P], F32, name="xt")
                for g in range(PASSES):
                    for u in range(PAIR):
                        first = (j * PASSES + g) * PAIR * P
                        if c in sorted_tiles and j in SORTED_TILES:
                            words = sorted_tiles[c][:, SORTED_TILES.index(j), g, u, :]
                        else:
                            words = x_words[:, first + u : first + PAIR * P : PAIR]
                        nc.tensor.transpose(out=xt[:, g, u, :], in_=words, identity=ident[:])
                nc.scalar.copy(out=grouped_words[:, j], in_=xt[:].rearrange("p g u r -> p g r u"))

        def quantise(c, tiles=range(TILES)):
            if tiles[0] == 0:
                words = TILES * PASSES * P
                code_tiles[c] = mx_pool.tile([P, words], U32, name="x_codes", align_bytes=64)
                scale_tiles[c] = mx_pool.tile([P, words], U8, name="x_scales", align_bytes=64)
            first, end = tiles[0] * PASSES * P, (tiles[-1] + 1) * PASSES * P
            nc.vector.quantize_mx(
                out=code_tiles[c][:, first:end].bitcast(FP8X4),
                scales=scale_tiles[c][:, first:end],
                in_=grouped_tiles[c][:, first * PACK : end * PACK],
            )

        def project(c, name, tiles, weight):
            w_codes, w_scales, cols = w_operands[weight]
            acc = head_psum.tile([P, len(tiles) * cols], F32, name=name)
            for i, j in enumerate(tiles):
                for g in range(PASSES):
                    tokens = slice((j * PASSES + g) * P, (j * PASSES + g + 1) * P)
                    columns = slice(g * cols, (g + 1) * cols)
                    nc.tensor.matmul_mx(
                        out=acc[:, i * cols : (i + 1) * cols],
                        lhsT=code_tiles[c][:, tokens].bitcast(FP8X4),
                        lhsT_scale=scale_tiles[c][:, tokens],
                        rhs=w_codes[:, columns].bitcast(FP8X4),
                        rhs_scale=w_scales[:, columns],
                        start=(g == 0),
                        stop=(g == PASSES - 1),
                    )
            head_tiles[c, name] = acc

        def project_q(c, b):
            project(c, "q%d" % b, BANK_TILES[b], "q")

        def project_k(c):
            project(c, "k", range(TILES), "k")

        def project_v(c):
            project(c, "v", range(TILES), "v")

        def store_v(c):
            v_out = out_pool.tile([P, TILES * HEAD], F32, name="v_out")
            nc.scalar.copy(out=v_out[:], in_=head_tiles[c, "v"][:])
            nc.sync.dma_start(out=v_chunks[c], in_=v_out[:])

        def multiply_q(c, b):
            if b == 0:
                product_tiles[c] = out_pool.tile([P, 2, ROT_VECTORS, HEAD], F32, name="products")
            vectors = Q_BANK_TILES * Q_HEADS
            shape = [P, 2, Q_BANK_TILES, Q_HEADS, HEAD]
            nc.vector.tensor_tensor(
                out=product_tiles[c][:, :, b * vectors : (b + 1) * vectors, :].rearrange(
                    "p w (j h) d -> p w j h d", h=Q_HEADS
                ),
                in0=head_tiles[c, "q%d" % b][:]
                .rearrange("p (j h d) -> p j h d", h=Q_HEADS, d=HEAD)
                .unsqueeze(1)
                .to_broadcast(shape),
                in1=tables[:, (c % SEQ_CHUNKS) * Q_BANKS + b]
                .rearrange("p w (j d) -> p w j d", d=HEAD)
                .unsqueeze(3)
                .to_broadcast(shape),
                op=ALU.mult,
            )

        def multiply_k(c):
            first = (c % SEQ_CHUNKS) * Q_BANKS
            shape = [P, 2, Q_BANKS, Q_BANK_TILES * HEAD]
            nc.vector.tensor_tensor(
                out=product_tiles[c][:, :, Q_VECTORS:ROT_VECTORS, :].rearrange(
                    "p w (b j) d -> p w b (j d)", b=Q_BANKS
                ),
                in0=head_tiles[c, "k"][:].rearrange("p (b n) -> p b n", b=Q_BANKS).unsqueeze(1).to_broadcast(shape),
                in1=tables[:, first : first + Q_BANKS].rearrange("p b w n -> p w b n"),
                op=ALU.mult,
            )

        def add(c, engine, first, end):
            if first == 0:
                rot_tiles[c] = out_pool.tile([P, ROT_VECTORS, HEAD], F32, name="rot")
            vectors = product_tiles[c][:, :, first:end, :].rearrange("p w n (f d) -> p w n f d", f=2)
            engine.tensor_tensor(
                out=rot_tiles[c][:, first:end, :].rearrange("p n (f d) -> p n f d", f=2),
                in0=vectors[:, 0],
                in1=vectors[:, 1, :, ::-1, :],
                op=ALU.add,
            )

        def store_q(c, first=0, end=Q_VECTORS):
            rot = rot_tiles[c][:, first:end, :]
            nc.sync.dma_start(
                out=q_chunks[c][:, first * HEAD : end * HEAD], in_=rot.rearrange("p n d -> p (n d)")
            )

        def store_k(c):
            rot = rot_tiles[c][:, Q_VECTORS:ROT_VECTORS, :]
            nc.sync.dma_start(out=k_chunks[c], in_=rot.rearrange("p n d -> p (n d)"))

        ident = const.tile([P, P], F32)
        make_identity(nc, ident[:])

        table_rows = Q_BANK_TILES * HEAD
        tables = const.tile([P, SEQ_CHUNKS * Q_BANKS, 2, table_rows], BF16)
        sin_sb = const.tile([P, SEQ_CHUNKS * Q_BANKS, table_rows], BF16)

        def load_tables(first, end):
            banks = slice(first * Q_BANKS, end * Q_BANKS)
            for table_sb, table in ((sin_sb[:, banks], sin), (tables[:, banks, 0], cos)):
                by_bank = table.rearrange("(c p b j) d -> p c b (j d)", p=P, b=Q_BANKS, j=Q_BANK_TILES)
                for c in range(first, end):
                    b = (c - first) * Q_BANKS
                    nc.sync.dma_start(out=table_sb[:, b : b + Q_BANKS], in_=by_bank[:, c])

        def build_tables(c):
            banks = slice(c * Q_BANKS, (c + 1) * Q_BANKS)
            swapped = tables[:, banks, 1].rearrange("p b (j d) -> p b j d", d=HEAD)
            rows = sin_sb[:, banks].rearrange("p b (j d) -> p b j d", d=HEAD)
            nc.scalar.copy(out=swapped[:, :, :, 0:HALF], in_=rows[:, :, :, HALF:HEAD])
            nc.scalar.mul(swapped[:, :, :, HALF:HEAD], rows[:, :, :, 0:HALF], -1.0)

        w_raws, w_groups = {}, {}

        def load_weight(name, w, passes=range(PASSES)):
            if passes[0] == 0:
                w_raws[name] = const.tile([P, PASSES, PACK, w.shape[1]], BF16, name=name + "_raw")
            passes = slice(passes[0], passes[-1] + 1)
            nc.sync.dma_start(
                out=w_raws[name][:, passes].rearrange("p g t n -> p g (t n)"),
                in_=w.rearrange("(g q t) n -> q g (t n)", q=P, t=PACK)[:, passes],
            )

        def group_weight(name):
            w_raw = w_raws[name]
            shape = [P, PASSES, w_raw.shape[3], PACK]
            w_groups[name] = const.tile(shape, BF16, name=name + "_grouped", align_bytes=64)
            for g in range(PASSES):
                nc.vector.tensor_copy(out=w_groups[name][:, g], in_=w_raw[:, g].rearrange("p t n -> p n t"))

        def quantise_weight(name):
            cols = w_raws[name].shape[3]
            w_codes = const.tile([P, PASSES * cols], U32, name=name + "_codes", align_bytes=64)
            w_scales = const.tile([P, PASSES * cols], U8, name=name + "_scales", align_bytes=64)
            nc.vector.quantize_mx(
                out=w_codes[:].bitcast(FP8X4),
                scales=w_scales[:],
                in_=w_groups[name][:].rearrange("p g n t -> p (g n t)"),
            )
            w_operands[name] = (w_codes, w_scales, cols)

        early, late = BANK_TILES
        load_weight("q", Wq, range(0, 1))
        load(0, range(0, 1))
        load(0, range(1, 2))
        load_weight("q", Wq, range(1, 2))
        load(0, range(2, 3))
        load(0, range(3, 4))
        load_weight("k", Wk)
        load_tables(0, 1)
        load(1, early)
        load_weight("v", Wv)
        load(1, late)
        load_tables(1, 2)
        load(2)
        load(3)
        load_tables(2, SEQ_CHUNKS)
        load(4)
        load(5)

        transpose(0)
        build_tables(0)
        group_weight("q")
        quantise_weight("q")
        quantise(0, early)
        group_weight("k")
        project_q(0, 0)
        quantise_weight("k")
        multiply_q(0, 0)
        quantise(0, late)
        group_weight("v")
        quantise_weight("v")

        transpose(1, early)
        project_q(0, 1)
        multiply_q(0, 1)
        transpose(1, late)
        quantise(1, early)
        project_k(0)
        multiply_k(0)
        gpsimd_vectors = Q_VECTORS + 1
        add(0, nc.gpsimd, 0, gpsimd_vectors)
        quantise(1, late)
        build_tables(1)
        transpose(2, early)
        project_q(1, 0)
        multiply_q(1, 0)
        transpose(2, late)
        project_q(1, 1)
        multiply_q(1, 1)
        quantise(2)
        add(0, nc.vector, gpsimd_vectors, ROT_VECTORS)
        store_q(0)
        store_k(0)
        transpose(3)
        project_k(1)
        multiply_k(1)
        add(1, nc.gpsimd, 0, ROT_VECTORS)
        project_v(0)
        store_v(0)
        build_tables(2)

        for c in range(2, CHUNKS):
            if c + LOAD_AHEAD < CHUNKS:
                load(c + LOAD_AHEAD)
            if c + 1 < CHUNKS:
                quantise(c + 1)
            for b in range(Q_BANKS):
                project_q(c, b)
                multiply_q(c, b)
            if c == 2:
                project_v(1)
                store_v(1)
            if c + 2 < CHUNKS:
                transpose(c + 2)
            if c + SORT_AHEAD < CHUNKS:
                sort(c + SORT_AHEAD)
            store_q(c - 1)
            project_k(c)
            project_v(c)
            store_v(c)
            store_k(c - 1)
            multiply_k(c)
            if c < CHUNKS - 2:
                add(c, nc.gpsimd, 0, ROT_VECTORS)
            elif c == CHUNKS - 2:
                add(c, nc.gpsimd, 0, Q_VECTORS)
                add(c, nc.gpsimd, Q_VECTORS, ROT_VECTORS)
            if c + 1 < SEQ_CHUNKS:
                build_tables(c + 1)

        last = CHUNKS - 1
        half = Q_VECTORS // 2
        for first in (0, half):
            add(last, nc.vector, first, first + half)
            store_q(last, first, first + half)
        add(last, nc.vector, Q_VECTORS, ROT_VECTORS)
        store_k(last)
